import numpy as np
import ml_dtypes


def mxq(x, axis, fmt="e4m3"):
    dtype, down = {"e4m3": (ml_dtypes.float8_e4m3fn, 7), "e5m2": (ml_dtypes.float8_e5m2, 14)}[fmt]
    v = np.moveaxis(np.asarray(x, np.float32).astype(ml_dtypes.bfloat16).astype(np.float64), axis, -1)
    blocks = v.reshape(v.shape[:-1] + (-1, 32))
    amax = np.abs(blocks).max(-1, keepdims=True)
    byte = np.maximum(np.where(amax > 0, np.frexp(amax)[1] - 1 + 127, 0) - down, 1)
    scale = np.exp2(byte - 127.0)
    codes = (blocks / scale).astype(np.float32).astype(dtype).astype(np.float64)
    return np.moveaxis((codes * scale).reshape(v.shape), -1, axis)


WIDE = False


def mx_kscale(k):
    if not WIDE:
        return np.ones(k)
    levels = np.array([10, -10, 5, -5, 0])
    a = np.random.permutation(np.resize(levels, k // 512 * 4)).reshape(k // 512, 4)
    idx = np.arange(k)
    return np.exp2(a[idx // 512, idx % 128 // 32])


BF16 = ml_dtypes.bfloat16


def bf(x):
    return np.asarray(x, np.float32).astype(BF16)


def f64(x):
    return np.asarray(x).astype(np.float64)


B, K, N, H, W = 1, 4096, 1024, 32, 32
NUM_ITERS = 5
TEMP = 0.1


def logsumexp(a, axis):
    m = a.max(axis=axis, keepdims=True)
    return m + np.log(np.exp(a - m).sum(axis=axis, keepdims=True))


def setup_inputs():
    s = mx_kscale(H * W).reshape(H, W)
    return {"pred_masks": bf(np.random.standard_normal((B, K, H, W)) * s),
            "gt_masks": bf(np.random.standard_normal((N, H, W)) * 0.5 / np.sqrt(H * W) / s)}


def reference(pred_masks, gt_masks):
    p = f64(pred_masks).reshape(B, K, H * W)
    g = f64(gt_masks).reshape(N, H * W)
    dot = mxq(p, 2, "e4m3") @ mxq(g, 1, "e4m3").T
    cost = 1.0 - dot
    log_alpha = -cost / TEMP
    for _ in range(NUM_ITERS):
        log_alpha = log_alpha - logsumexp(log_alpha, 2)
        log_alpha = log_alpha - logsumexp(log_alpha, 1)
    return np.exp(log_alpha)

@@ -1,0 +1,320 @@
+from contextlib import ExitStack
+
+import concourse.bass as bass
+import concourse.mybir as mybir
+import concourse.tile as tile
+from concourse.masks import make_identity
+
+F32 = mybir.dt.float32
+BF16 = mybir.dt.bfloat16
+U32 = mybir.dt.uint32
+U8 = mybir.dt.uint8
+FP8X4 = mybir.dt.float8_e4m3fn_x4
+ALU = mybir.AluOpType
+ACT = mybir.ActivationFunctionType
+AX = mybir.AxisListType
+
+P = 128
+ROWS = 4096
+COLS = 1024
+CONTR = 1024
+RT = ROWS // P
+CC = COLS // P
+NP = 22
+NV = RT - NP
+ITERS = 5
+INV_TEMP = 10.0
+KB = 1024
+
+FLOPS = 2 * ROWS * COLS * CONTR
+
+OFF_EAH = 0
+OFF_EAL = OFF_EAH + NP * 2 * KB
+OFF_EB = OFF_EAL + NP * 2 * KB
+OFF_EV = OFF_EB + NP * 4 * KB
+OFF_MISC = OFF_EV + NV * 4 * KB
+OFF_GRAW = OFF_EAH + (NP - 8) * 2 * KB
+OFF_GGRP = OFF_EAL + (NP - 8) * 2 * KB
+OFF_GC = OFF_MISC
+OFF_GS = OFF_MISC + 8 * KB
+OFF_ACC = OFF_MISC
+OFF_ACCH = OFF_MISC + 4 * KB
+OFF_ACCL = OFF_MISC + 6 * KB
+OFF_JUNK = OFF_MISC + 8 * KB
+OFF_GRP = OFF_MISC + 10 * KB
+OFF_COD = OFF_MISC + 14 * KB
+OFF_PLN = OFF_MISC + 16 * KB
+
+
+def tile_differentiablematcher_t_kernel(tc, pred_masks, gt_masks, out):
+    nc = tc.nc
+    pv = pred_masks.rearrange("b (p t) h w -> (b p) t (h w)", t=RT)
+    gv = gt_masks.rearrange("(c p) h w -> p c (h w)", p=P)
+    ov = out.rearrange("b (p t) n -> (b p) t n", t=RT)
+
+    with ExitStack() as ctx:
+        big = ctx.enter_context(tc.tile_pool(name="big", bufs=1))
+        small = ctx.enter_context(tc.tile_pool(name="small", bufs=1))
+        tiny = ctx.enter_context(tc.tile_pool(name="tiny", bufs=4))
+        ps = ctx.enter_context(tc.psum_pool(name="ps", bufs=1))
+
+        def bank(b, shape, dtype, name):
+            return ps.tile(shape, dtype, name=name, tag="bk%d" % b)
+
+        g_raw = big.tile([P, CC, CONTR], BF16, name="g_raw", offset=OFF_GRAW)
+        for q in range(4):
+            nc.sync.dma_start(out=g_raw[:, 2 * q:2 * q + 2, :], in_=gv[:, 2 * q:2 * q + 2, :])
+        p_raw = []
+        for n in range(RT // 2):
+            if 2 * n < NP:
+                off = OFF_EB + 2 * n * 4 * KB
+            else:
+                off = OFF_EV + (2 * n - NP + 1) * 4 * KB
+            r = big.tile([P, 2, CONTR], BF16, name="p_raw%d" % n, offset=off)
+            nc.sync.dma_start(out=r[:], in_=pv[:, 2 * n:2 * n + 2, :])
+            p_raw.append(r)
+
+        ident_f = small.tile([P, P], F32, name="ident_f")
+        make_identity(nc, ident_f[:])
+        ident_b = small.tile([P, P], BF16, name="ident_b")
+        make_identity(nc, ident_b[:])
+        onescol = small.tile([P, 2], BF16, name="onescol")
+        nc.vector.memset(onescol[:, 0:1], 1.0)
+        nc.vector.memset(onescol[:, 1:2], 0.0)
+        mva = small.tile([P, NP, 2], BF16, name="mva")
+        mvb = small.tile([P, CC, 2], BF16, name="mvb")
+        rs = small.tile([P, RT, 2], F32, name="rs")
+        s_all = small.tile([P, RT], F32, name="s_all")
+        a_all = small.tile([P, RT], F32, name="a_all")
+        svh = small.tile([P, NV, 2], F32, name="svh")
+        tt = small.tile([P, CC], F32, name="tt")
+        bv = small.tile([P, CC], F32, name="bv")
+
+        g_grp = big.tile([P, 2, 4 * COLS], BF16, name="g_grp", offset=OFF_GGRP, align_bytes=64)
+        g_grp_w = g_grp[:].bitcast(F32).rearrange("p g (j u) -> p g j u", u=2)
+        gc = big.tile([P, 2, COLS], U32, name="gc", offset=OFF_GC, align_bytes=64)
+        gs = big.tile([P, 2, COLS], U8, name="gs", offset=OFF_GS, align_bytes=64)
+        for jc in range(CC):
+            tpg = bank(jc, [P, 2, 2, P], F32, "tpg")
+            src = g_raw[:, jc, :].bitcast(F32)
+            for g in range(2):
+                for u in range(2):
+                    lo = 256 * g + 128 * u
+                    nc.tensor.transpose(tpg[:, g, u, :], src[:, lo:lo + P], ident_f[:])
+            dst = g_grp_w[:, :, jc * P:(jc + 1) * P, :]
+            if jc % 2 == 0:
+                nc.vector.tensor_copy(out=dst, in_=tpg[:].rearrange("p g u w -> p g w u"))
+            else:
+                nc.scalar.copy(out=dst, in_=tpg[:].rearrange("p g u w -> p g w u"))
+        for half in range(2):
+            for g in range(2):
+                nc.vector.quantize_mx(
+                    out=gc[:, g, half * 512:(half + 1) * 512].bitcast(FP8X4),
+                    scales=gs[:, g, half * 512:(half + 1) * 512],
+                    in_=g_grp[:, g, half * 2048:(half + 1) * 2048],
+                )
+
+        grp_of = {}
+        d_of = {}
+        eah = {}
+        eal = {}
+        ebh = {}
+        ebl = {}
+        ev = {}
+
+        def stage_t(t):
+            src = p_raw[t // 2][:, t % 2, :].bitcast(F32)
+            tp = bank(t % 2, [P, 2, 2, P], F32, "tp")
+            for g in range(2):
+                for u in range(2):
+                    lo = 256 * g + 128 * u
+                    nc.tensor.transpose(tp[:, g, u, :], src[:, lo:lo + P], ident_f[:])
+            grp = big.tile([P, 4 * 256], BF16, name="grp%d" % (t % 2),
+                           offset=OFF_GRP + (t % 2) * 2 * KB, align_bytes=64)
+            nc.scalar.copy(
+                out=grp[:].bitcast(F32).rearrange("p (g i u) -> p g i u", g=2, u=2),
+                in_=tp[:].rearrange("p g u i -> p g i u"),
+            )
+            grp_of[t] = grp
+
+        def stage_q(t):
+            cod = big.tile([P, 256], U32, name="cod%d" % (t % 2),
+                           offset=OFF_COD + (t % 2) * KB, align_bytes=64)
+            pln = big.tile([P, 256], U8, name="pln%d" % (t % 2),
+                           offset=OFF_PLN + (t % 2) * 256, align_bytes=64)
+            nc.vector.quantize_mx(out=cod[:].bitcast(FP8X4), scales=pln[:], in_=grp_of[t][:])
+            ds = []
+            for h in range(2):
+                d = bank(2 + 2 * (t % 2) + h, [P, 512], F32, "d")
+                for g in range(2):
+                    nc.tensor.matmul_mx(
+                        out=d[:],
+                        lhsT=cod[:, g * P:(g + 1) * P].bitcast(FP8X4),
+                        lhsT_scale=pln[:, g * P:(g + 1) * P],
+                        rhs=gc[:, g, h * 512:(h + 1) * 512].bitcast(FP8X4),
+                        rhs_scale=gs[:, g, h * 512:(h + 1) * 512],
+                        start=(g == 0),
+                        stop=(g == 1),
+                    )
+                ds.append(d)
+            d_of[t] = ds
+
+        def stage_e(t):
+            ds = d_of[t]
+            m2 = tiny.tile([P, 2], F32, name="m2")
+            for h in range(2):
+                nc.vector.tensor_reduce(out=m2[:, h:h + 1], in_=ds[h][:], axis=AX.X, op=ALU.max)
+            nb = tiny.tile([P, 1], F32, name="nb")
+            nc.vector.tensor_scalar(out=nb[:], in0=m2[:, 0:1], scalar1=m2[:, 1:2],
+                                    scalar2=-INV_TEMP, op0=ALU.max, op1=ALU.mult)
+            if t < NP:
+                dest = big.tile([P, COLS], F32, name="e32_%d" % (t % 3),
+                                offset=OFF_EV + (t % 3) * 8 * KB)
+            else:
+                dest = big.tile([P, COLS], F32, name="ev%d" % (t - NP),
+                                offset=OFF_EV + (t - NP) * 4 * KB)
+                ev[t - NP] = dest
+            for h in range(2):
+                nc.scalar.activation(out=dest[:, h * 512:(h + 1) * 512], in_=ds[h][:], func=ACT.Exp,
+                                     bias=nb[:, 0:1], scale=INV_TEMP, accum_out=rs[:, t, h:h + 1])
+            if t < NP:
+                nc.sync.dma_start(out=ov[:, t, :], in_=dest[:])
+                hi = big.tile([P, COLS], BF16, name="eah%d" % t, offset=OFF_EAH + t * 2 * KB)
+                nc.gpsimd.tensor_scalar(out=hi[:], in0=dest[:], scalar1=1.0, scalar2=0.0,
+                                        op0=ALU.mult, op1=ALU.add)
+                lo = big.tile([P, COLS], BF16, name="eal%d" % t, offset=OFF_EAL + t * 2 * KB)
+                nc.vector.tensor_tensor(out=lo[:], in0=dest[:], in1=hi[:], op=ALU.subtract)
+                eah[t] = hi
+                eal[t] = lo
+
+        def stage_b(t):
+            for part in range(2):
+                src = eah[t] if part == 0 else eal[t]
+                ebp = bank(6 + part, [P, CC, P], BF16, "ebp")
+                for jc in range(CC):
+                    nc.tensor.transpose(ebp[:, jc, :], src[:, jc * P:(jc + 1) * P], ident_b[:])
+                eb = big.tile([P, CC, P], BF16, name="eb%d_%d" % (part, t),
+                              offset=OFF_EB + t * 4 * KB + part * 2 * KB)
+                nc.scalar.copy(out=eb[:], in_=ebp[:])
+                if part == 0:
+                    ebh[t] = eb
+                else:
+                    ebl[t] = eb
+
+        for s in range(RT + 3):
+            if 0 <= s - 1 < RT:
+                stage_q(s - 1)
+            if 0 <= s - 3 < NP:
+                stage_b(s - 3)
+            if s < RT:
+                stage_t(s)
+            if 0 <= s - 2 < RT:
+                stage_e(s - 2)
+
+        acc = big.tile([P, COLS], F32, name="acc", offset=OFF_ACC)
+        acch = big.tile([P, COLS], BF16, name="acch", offset=OFF_ACCH)
+        accl = big.tile([P, COLS], BF16, name="accl", offset=OFF_ACCL)
+        junk = big.tile([P, 512], F32, name="junk", offset=OFF_JUNK)
+
+        def split(mv, vec):
+            nc.vector.tensor_copy(out=mv[:, :, 0:1], in_=vec.unsqueeze(2))
+            nc.vector.tensor_tensor(out=mv[:, :, 1:2], in0=vec.unsqueeze(2), in1=mv[:, :, 0:1],
+                                    op=ALU.subtract)
+
+        def broadcast_bv():
+            bc = []
+            for h in range(2):
+                b = bank(2 + h, [P, 512], F32, "bc")
+                bc.append(b)
+            for jc in range(CC):
+                o = bc[jc // 4][:, (jc % 4) * P:(jc % 4 + 1) * P]
+                nc.tensor.matmul(o, lhsT=mvb[:, jc, 0:1].to_broadcast([P, P]), rhs=ident_b[:],
+                                 start=True, stop=False)
+                nc.tensor.matmul(o, lhsT=mvb[:, jc, 1:2].to_broadcast([P, P]), rhs=ident_b[:],
+                                 start=False, stop=True)
+            return bc
+
+        def row_step():
+            bc = broadcast_bv()
+            rsp = bank(4, [P, NP, 2], F32, "rsp")
+            for t in range(NP):
+                k = 0
+                for jc in range(CC):
+                    for eb in (ebh[t], ebl[t]):
+                        nc.tensor.matmul(rsp[:, t, :], lhsT=eb[:, jc, :], rhs=mvb[:, jc, :],
+                                         start=(k == 0), stop=(k == 2 * CC - 1))
+                        k += 1
+            for v in range(NV):
+                for h in range(2):
+                    nc.vector.scalar_tensor_tensor(
+                        out=junk[:], in0=ev[v][:, h * 512:(h + 1) * 512], scalar=1.0, in1=bc[h][:],
+                        op0=ALU.mult, op1=ALU.mult, accum_out=svh[:, v, h:h + 1])
+            nc.vector.tensor_reduce(out=s_all[:, 0:NP], in_=rsp[:], axis=AX.X, op=ALU.add)
+            nc.vector.tensor_reduce(out=s_all[:, NP:RT], in_=svh[:], axis=AX.X, op=ALU.add)
+
+        def col_step():
+            nc.vector.reciprocal(out=a_all[:, 0:NP], in_=s_all[:, 0:NP])
+            split(mva, a_all[:, 0:NP])
+            nc.vector.reciprocal(out=a_all[:, NP:RT], in_=s_all[:, NP:RT])
+            csp = bank(6, [P, CC, 2, 2], F32, "csp")
+            for jc in range(CC):
+                k = 0
+                for t in range(NP):
+                    for ea in (eah[t], eal[t]):
+                        nc.tensor.matmul(csp[:, jc, 0, :], lhsT=ea[:, jc * P:(jc + 1) * P],
+                                         rhs=mva[:, t, :], start=(k == 0), stop=(k == 2 * NP - 1))
+                        k += 1
+            for v in range(NV):
+                for h in range(2):
+                    hs = slice(h * 512, (h + 1) * 512)
+                    if v == 0:
+                        nc.vector.tensor_scalar(out=acc[:, hs], in0=ev[v][:, hs],
+                                                scalar1=a_all[:, NP:NP + 1], scalar2=None,
+                                                op0=ALU.mult)
+                    else:
+                        nc.vector.scalar_tensor_tensor(
+                            out=acc[:, hs], in0=ev[v][:, hs], scalar=a_all[:, NP + v:NP + v + 1],
+                            in1=acc[:, hs], op0=ALU.mult, op1=ALU.add)
+            for h in range(2):
+                hs = slice(h * 512, (h + 1) * 512)
+                nc.vector.tensor_copy(out=acch[:, hs], in_=acc[:, hs])
+                nc.vector.tensor_tensor(out=accl[:, hs], in0=acc[:, hs], in1=acch[:, hs],
+                                        op=ALU.subtract)
+            for jc in range(CC):
+                nc.tensor.matmul(csp[:, jc, 1, :], lhsT=acch[:, jc * P:(jc + 1) * P], rhs=onescol[:],
+                                 start=True, stop=False)
+                nc.tensor.matmul(csp[:, jc, 1, :], lhsT=accl[:, jc * P:(jc + 1) * P], rhs=onescol[:],
+                                 start=False, stop=True)
+            nc.vector.tensor_reduce(out=tt[:], in_=csp[:], axis=AX.XY, op=ALU.add)
+            nc.vector.reciprocal(out=bv[:], in_=tt[:])
+            split(mvb, bv[:])
+
+        nc.vector.tensor_reduce(out=s_all[:], in_=rs[:], axis=AX.X, op=ALU.add)
+        r32 = {}
+        for it in range(ITERS):
+            if it > 0:
+                row_step()
+            if it == ITERS - 1:
+                for t in range(0, NP, 2):
+                    r = big.tile([P, 2, COLS], F32, name="r32_%d" % t, offset=OFF_EB + t * 4 * KB)
+                    nc.sync.dma_start(out=r[:], in_=ov[:, t:t + 2, :])
+                    r32[t] = r
+            col_step()
+
+        bc = broadcast_bv()
+        for v in range(NV):
+            for h in range(2):
+                hs = slice(h * 512, (h + 1) * 512)
+                nc.vector.scalar_tensor_tensor(
+                    out=ev[v][:, hs], in0=ev[v][:, hs], scalar=a_all[:, NP + v:NP + v + 1],
+                    in1=bc[h][:], op0=ALU.mult, op1=ALU.mult)
+            nc.sync.dma_start(out=ov[:, NP + v, :], in_=ev[v][:])
+        for t in range(0, NP, 2):
+            for e in range(2):
+                for h in range(2):
+                    hs = slice(h * 512, (h + 1) * 512)
+                    nc.vector.scalar_tensor_tensor(
+                        out=r32[t][:, e, hs], in0=r32[t][:, e, hs],
+                        scalar=a_all[:, t + e:t + e + 1], in1=bc[h][:],
+                        op0=ALU.mult, op1=ALU.mult)
+            nc.sync.dma_start(out=ov[:, t:t + 2, :], in_=r32[t][:])

@@ -1,8 +1,6 @@
 from contextlib import ExitStack
 
-import concourse.bass as bass
 import concourse.mybir as mybir
-import concourse.tile as tile
 from concourse.masks import make_identity
 
 F32 = mybir.dt.float32
@@ -22,10 +20,12 @@ RT = ROWS // P
 CC = COLS // P
 NP = 22
 NV = RT - NP
+NCOL = 2
 ITERS = 5
 INV_TEMP = 10.0
 KB = 1024
-
+EARLY = 2
+GPAIRS = 5
 FLOPS = 2 * ROWS * COLS * CONTR
 
 OFF_EAH = 0
@@ -57,6 +57,7 @@ def tile_differentiablematcher_t_kernel(tc, pred_masks, gt_masks, out):
         small = ctx.enter_context(tc.tile_pool(name="small", bufs=1))
         tiny = ctx.enter_context(tc.tile_pool(name="tiny", bufs=4))
         ps = ctx.enter_context(tc.psum_pool(name="ps", bufs=1))
+        ctx.enter_context(tc.manual_schedule())
 
         def bank(b, shape, dtype, name):
             return ps.tile(shape, dtype, name=name, tag="bk%d" % b)
@@ -78,11 +79,13 @@ def tile_differentiablematcher_t_kernel(tc, pred_masks, gt_masks, out):
         make_identity(nc, ident_f[:])
         ident_b = small.tile([P, P], BF16, name="ident_b")
         make_identity(nc, ident_b[:])
-        onescol = small.tile([P, 2], BF16, name="onescol")
+        onescol = small.tile([P, NCOL], BF16, name="onescol")
+        nc.vector.memset(onescol[:], 0.0)
         nc.vector.memset(onescol[:, 0:1], 1.0)
-        nc.vector.memset(onescol[:, 1:2], 0.0)
-        mva = small.tile([P, NP, 2], BF16, name="mva")
-        mvb = small.tile([P, CC, 2], BF16, name="mvb")
+        mva = small.tile([P, NP, NCOL], BF16, name="mva")
+        nc.vector.memset(mva[:], 0.0)
+        mvb = small.tile([P, CC, NCOL], BF16, name="mvb")
+        nc.vector.memset(mvb[:], 0.0)
         rs = small.tile([P, RT, 2], F32, name="rs")
         s_all = small.tile([P, RT], F32, name="s_all")
         a_all = small.tile([P, RT], F32, name="a_all")
@@ -94,19 +97,19 @@ def tile_differentiablematcher_t_kernel(tc, pred_masks, gt_masks, out):
         g_grp_w = g_grp[:].bitcast(F32).rearrange("p g (j u) -> p g j u", u=2)
         gc = big.tile([P, 2, COLS], U32, name="gc", offset=OFF_GC, align_bytes=64)
         gs = big.tile([P, 2, COLS], U8, name="gs", offset=OFF_GS, align_bytes=64)
-        for jc in range(CC):
-            tpg = bank(jc, [P, 2, 2, P], F32, "tpg")
-            src = g_raw[:, jc, :].bitcast(F32)
-            for g in range(2):
-                for u in range(2):
-                    lo = 256 * g + 128 * u
-                    nc.tensor.transpose(tpg[:, g, u, :], src[:, lo:lo + P], ident_f[:])
-            dst = g_grp_w[:, :, jc * P:(jc + 1) * P, :]
-            if jc % 2 == 0:
-                nc.vector.tensor_copy(out=dst, in_=tpg[:].rearrange("p g u w -> p g w u"))
-            else:
-                nc.scalar.copy(out=dst, in_=tpg[:].rearrange("p g u w -> p g w u"))
         for half in range(2):
+            for jc in range(4 * half, 4 * half + 4):
+                tpg = bank(jc, [P, 2, 2, P], F32, "tpg")
+                src = g_raw[:, jc, :].bitcast(F32)
+                for g in range(2):
+                    for u in range(2):
+                        lo = 256 * g + 128 * u
+                        nc.tensor.transpose(tpg[:, g, u, :], src[:, lo:lo + P], ident_f[:])
+                dst = g_grp_w[:, :, jc * P:(jc + 1) * P, :]
+                if jc % 2 == 0:
+                    nc.vector.tensor_copy(out=dst, in_=tpg[:].rearrange("p g u w -> p g w u"))
+                else:
+                    nc.scalar.copy(out=dst, in_=tpg[:].rearrange("p g u w -> p g w u"))
             for g in range(2):
                 nc.vector.quantize_mx(
                     out=gc[:, g, half * 512:(half + 1) * 512].bitcast(FP8X4),
@@ -115,14 +118,18 @@ def tile_differentiablematcher_t_kernel(tc, pred_masks, gt_masks, out):
                 )
 
         grp_of = {}
+        cod_of = {}
         d_of = {}
+        nb_of = {}
+        e32_of = {}
         eah = {}
         eal = {}
+        ebp_of = {}
         ebh = {}
         ebl = {}
         ev = {}
 
-        def stage_t(t):
+        def do_transposes(t):
             src = p_raw[t // 2][:, t % 2, :].bitcast(F32)
             tp = bank(t % 2, [P, 2, 2, P], F32, "tp")
             for g in range(2):
@@ -137,12 +144,16 @@ def tile_differentiablematcher_t_kernel(tc, pred_masks, gt_masks, out):
             )
             grp_of[t] = grp
 
-        def stage_q(t):
+        def do_quantise(t):
             cod = big.tile([P, 256], U32, name="cod%d" % (t % 2),
                            offset=OFF_COD + (t % 2) * KB, align_bytes=64)
             pln = big.tile([P, 256], U8, name="pln%d" % (t % 2),
                            offset=OFF_PLN + (t % 2) * 256, align_bytes=64)
             nc.vector.quantize_mx(out=cod[:].bitcast(FP8X4), scales=pln[:], in_=grp_of[t][:])
+            cod_of[t] = (cod, pln)
+
+        def do_mx(t):
+            cod, pln = cod_of[t]
             ds = []
             for h in range(2):
                 d = bank(2 + 2 * (t % 2) + h, [P, 512], F32, "d")
@@ -159,7 +170,7 @@ def tile_differentiablematcher_t_kernel(tc, pred_masks, gt_masks, out):
                 ds.append(d)
             d_of[t] = ds
 
-        def stage_e(t):
+        def do_max(t):
             ds = d_of[t]
             m2 = tiny.tile([P, 2], F32, name="m2")
             for h in range(2):
@@ -167,49 +178,81 @@ def tile_differentiablematcher_t_kernel(tc, pred_masks, gt_masks, out):
             nb = tiny.tile([P, 1], F32, name="nb")
             nc.vector.tensor_scalar(out=nb[:], in0=m2[:, 0:1], scalar1=m2[:, 1:2],
                                     scalar2=-INV_TEMP, op0=ALU.max, op1=ALU.mult)
+            nb_of[t] = nb
+
+        def do_exp(t):
+            ds = d_of[t]
             if t < NP:
                 dest = big.tile([P, COLS], F32, name="e32_%d" % (t % 3),
                                 offset=OFF_EV + (t % 3) * 8 * KB)
+                e32_of[t] = dest
             else:
                 dest = big.tile([P, COLS], F32, name="ev%d" % (t - NP),
                                 offset=OFF_EV + (t - NP) * 4 * KB)
                 ev[t - NP] = dest
             for h in range(2):
                 nc.scalar.activation(out=dest[:, h * 512:(h + 1) * 512], in_=ds[h][:], func=ACT.Exp,
-                                     bias=nb[:, 0:1], scale=INV_TEMP, accum_out=rs[:, t, h:h + 1])
+                                     bias=nb_of[t][:, 0:1], scale=INV_TEMP,
+                                     accum_out=rs[:, t, h:h + 1])
             if t < NP:
                 nc.sync.dma_start(out=ov[:, t, :], in_=dest[:])
-                hi = big.tile([P, COLS], BF16, name="eah%d" % t, offset=OFF_EAH + t * 2 * KB)
-                nc.gpsimd.tensor_scalar(out=hi[:], in0=dest[:], scalar1=1.0, scalar2=0.0,
-                                        op0=ALU.mult, op1=ALU.add)
-                lo = big.tile([P, COLS], BF16, name="eal%d" % t, offset=OFF_EAL + t * 2 * KB)
-                nc.vector.tensor_tensor(out=lo[:], in0=dest[:], in1=hi[:], op=ALU.subtract)
-                eah[t] = hi
-                eal[t] = lo
 
-        def stage_b(t):
+        def do_cast(t):
+            hi = big.tile([P, COLS], BF16, name="eah%d" % t, offset=OFF_EAH + t * 2 * KB)
+            nc.gpsimd.tensor_scalar(out=hi[:], in0=e32_of[t][:], scalar1=1.0, scalar2=0.0,
+                                    op0=ALU.mult, op1=ALU.add)
+            eah[t] = hi
+
+        def do_sub(t, eng):
+            lo = big.tile([P, COLS], BF16, name="eal%d" % t, offset=OFF_EAL + t * 2 * KB)
+            eng.tensor_tensor(out=lo[:], in0=e32_of[t][:], in1=eah[t][:], op=ALU.subtract)
+            eal[t] = lo
+
+        def do_eb_transposes(t):
+            pair = []
             for part in range(2):
                 src = eah[t] if part == 0 else eal[t]
                 ebp = bank(6 + part, [P, CC, P], BF16, "ebp")
                 for jc in range(CC):
                     nc.tensor.transpose(ebp[:, jc, :], src[:, jc * P:(jc + 1) * P], ident_b[:])
+                pair.append(ebp)
+            ebp_of[t] = pair
+
+        def do_eb_copy(t):
+            for part in range(2):
                 eb = big.tile([P, CC, P], BF16, name="eb%d_%d" % (part, t),
                               offset=OFF_EB + t * 4 * KB + part * 2 * KB)
-                nc.scalar.copy(out=eb[:], in_=ebp[:])
+                if part == 1 and t % 2 == 0:
+                    nc.vector.tensor_copy(out=eb[:], in_=ebp_of[t][part][:])
+                else:
+                    nc.scalar.copy(out=eb[:], in_=ebp_of[t][part][:])
                 if part == 0:
                     ebh[t] = eb
                 else:
                     ebl[t] = eb
 
-        for s in range(RT + 3):
+        def sub_on_gpsimd(t):
+            return t % 3 == 1
+
+        for s in range(-2, RT + 4):
+            if 0 <= s - 2 < NP and not sub_on_gpsimd(s - 2):
+                do_sub(s - 2, nc.vector)
             if 0 <= s - 1 < RT:
-                stage_q(s - 1)
+                do_exp(s - 1)
+            if 0 <= s - 1 < NP:
+                do_cast(s - 1)
+                if sub_on_gpsimd(s - 1):
+                    do_sub(s - 1, nc.gpsimd)
+            if 0 <= s < RT:
+                do_mx(s)
+                do_max(s)
             if 0 <= s - 3 < NP:
-                stage_b(s - 3)
-            if s < RT:
-                stage_t(s)
-            if 0 <= s - 2 < RT:
-                stage_e(s - 2)
+                do_eb_transposes(s - 3)
+                do_eb_copy(s - 3)
+            if 0 <= s + 1 < RT:
+                do_quantise(s + 1)
+            if 0 <= s + 2 < RT:
+                do_transposes(s + 2)
 
         acc = big.tile([P, COLS], F32, name="acc", offset=OFF_ACC)
         acch = big.tile([P, COLS], BF16, name="acch", offset=OFF_ACCH)
@@ -234,29 +277,54 @@ def tile_differentiablematcher_t_kernel(tc, pred_masks, gt_masks, out):
                                  start=False, stop=True)
             return bc
 
-        def row_step():
-            bc = broadcast_bv()
-            rsp = bank(4, [P, NP, 2], F32, "rsp")
-            for t in range(NP):
-                k = 0
-                for jc in range(CC):
-                    for eb in (ebh[t], ebl[t]):
-                        nc.tensor.matmul(rsp[:, t, :], lhsT=eb[:, jc, :], rhs=mvb[:, jc, :],
-                                         start=(k == 0), stop=(k == 2 * CC - 1))
-                        k += 1
-            for v in range(NV):
-                for h in range(2):
-                    nc.vector.scalar_tensor_tensor(
-                        out=junk[:], in0=ev[v][:, h * 512:(h + 1) * 512], scalar=1.0, in1=bc[h][:],
-                        op0=ALU.mult, op1=ALU.mult, accum_out=svh[:, v, h:h + 1])
-            nc.vector.tensor_reduce(out=s_all[:, 0:NP], in_=rsp[:], axis=AX.X, op=ALU.add)
-            nc.vector.tensor_reduce(out=s_all[:, NP:RT], in_=svh[:], axis=AX.X, op=ALU.add)
+        def acc_step(v, h):
+            hs = slice(h * 512, (h + 1) * 512)
+            if v == 0:
+                nc.vector.tensor_scalar(out=acc[:, hs], in0=ev[v][:, hs],
+                                        scalar1=a_all[:, NP:NP + 1], scalar2=None, op0=ALU.mult)
+            else:
+                nc.vector.scalar_tensor_tensor(
+                    out=acc[:, hs], in0=ev[v][:, hs], scalar=a_all[:, NP + v:NP + v + 1],
+                    in1=acc[:, hs], op0=ALU.mult, op1=ALU.add)
 
-        def col_step():
-            nc.vector.reciprocal(out=a_all[:, 0:NP], in_=s_all[:, 0:NP])
-            split(mva, a_all[:, 0:NP])
-            nc.vector.reciprocal(out=a_all[:, NP:RT], in_=s_all[:, NP:RT])
-            csp = bank(6, [P, CC, 2, 2], F32, "csp")
+        r32 = {}
+        for it in range(ITERS):
+            if it == 0:
+                nc.vector.tensor_reduce(out=s_all[:], in_=rs[:], axis=AX.X, op=ALU.add)
+                nc.vector.reciprocal(out=a_all[:, 0:NP], in_=s_all[:, 0:NP])
+                split(mva, a_all[:, 0:NP])
+                nc.vector.reciprocal(out=a_all[:, NP:RT], in_=s_all[:, NP:RT])
+                early = 0
+            else:
+                bc = broadcast_bv()
+                rsp = bank(4, [P, NP, NCOL], F32, "rsp")
+                for t in range(NP):
+                    k = 0
+                    for jc in range(CC):
+                        for eb in (ebh[t], ebl[t]):
+                            nc.tensor.matmul(rsp[:, t, :], lhsT=eb[:, jc, :], rhs=mvb[:, jc, :],
+                                             start=(k == 0), stop=(k == 2 * CC - 1))
+                            k += 1
+                for v in range(NV):
+                    for h in range(2):
+                        nc.vector.scalar_tensor_tensor(
+                            out=junk[:], in0=ev[v][:, h * 512:(h + 1) * 512], scalar=1.0,
+                            in1=bc[h][:], op0=ALU.mult, op1=ALU.mult,
+                            accum_out=svh[:, v, h:h + 1])
+                nc.vector.tensor_reduce(out=s_all[:, NP:RT], in_=svh[:], axis=AX.X, op=ALU.add)
+                nc.vector.reciprocal(out=a_all[:, NP:RT], in_=s_all[:, NP:RT])
+                early = EARLY
+                for i in range(early):
+                    acc_step(i // 2, i % 2)
+                nc.vector.tensor_reduce(out=s_all[:, 0:NP], in_=rsp[:, :, 0:2], axis=AX.X, op=ALU.add)
+                nc.vector.reciprocal(out=a_all[:, 0:NP], in_=s_all[:, 0:NP])
+                split(mva, a_all[:, 0:NP])
+            if it == ITERS - 1:
+                for t in range(0, NP, 2):
+                    r = big.tile([P, 2, COLS], F32, name="r32_%d" % t, offset=OFF_EB + t * 4 * KB)
+                    nc.sync.dma_start(out=r[:], in_=ov[:, t:t + 2, :])
+                    r32[t] = r
+            csp = bank(6, [P, CC, 2, NCOL], F32, "csp")
             for jc in range(CC):
                 k = 0
                 for t in range(NP):
@@ -264,44 +332,37 @@ def tile_differentiablematcher_t_kernel(tc, pred_masks, gt_masks, out):
                         nc.tensor.matmul(csp[:, jc, 0, :], lhsT=ea[:, jc * P:(jc + 1) * P],
                                          rhs=mva[:, t, :], start=(k == 0), stop=(k == 2 * NP - 1))
                         k += 1
-            for v in range(NV):
-                for h in range(2):
-                    hs = slice(h * 512, (h + 1) * 512)
-                    if v == 0:
-                        nc.vector.tensor_scalar(out=acc[:, hs], in0=ev[v][:, hs],
-                                                scalar1=a_all[:, NP:NP + 1], scalar2=None,
-                                                op0=ALU.mult)
-                    else:
-                        nc.vector.scalar_tensor_tensor(
-                            out=acc[:, hs], in0=ev[v][:, hs], scalar=a_all[:, NP + v:NP + v + 1],
-                            in1=acc[:, hs], op0=ALU.mult, op1=ALU.add)
+            for i in range(early, 2 * NV):
+                acc_step(i // 2, i % 2)
             for h in range(2):
                 hs = slice(h * 512, (h + 1) * 512)
                 nc.vector.tensor_copy(out=acch[:, hs], in_=acc[:, hs])
                 nc.vector.tensor_tensor(out=accl[:, hs], in0=acc[:, hs], in1=acch[:, hs],
                                         op=ALU.subtract)
-            for jc in range(CC):
-                nc.tensor.matmul(csp[:, jc, 1, :], lhsT=acch[:, jc * P:(jc + 1) * P], rhs=onescol[:],
-                                 start=True, stop=False)
-                nc.tensor.matmul(csp[:, jc, 1, :], lhsT=accl[:, jc * P:(jc + 1) * P], rhs=onescol[:],
-                                 start=False, stop=True)
-            nc.vector.tensor_reduce(out=tt[:], in_=csp[:], axis=AX.XY, op=ALU.add)
+                for jc in range(4 * h, 4 * h + 4):
+                    nc.tensor.matmul(csp[:, jc, 1, :], lhsT=acch[:, jc * P:(jc + 1) * P],
+                                     rhs=onescol[:], start=True, stop=False)
+                    nc.tensor.matmul(csp[:, jc, 1, :], lhsT=accl[:, jc * P:(jc + 1) * P],
+                                     rhs=onescol[:], start=False, stop=True)
+            nc.vector.tensor_reduce(out=tt[:], in_=csp[:, :, :, 0:2], axis=AX.XY, op=ALU.add)
             nc.vector.reciprocal(out=bv[:], in_=tt[:])
             split(mvb, bv[:])
 
-        nc.vector.tensor_reduce(out=s_all[:], in_=rs[:], axis=AX.X, op=ALU.add)
-        r32 = {}
-        for it in range(ITERS):
-            if it > 0:
-                row_step()
-            if it == ITERS - 1:
-                for t in range(0, NP, 2):
-                    r = big.tile([P, 2, COLS], F32, name="r32_%d" % t, offset=OFF_EB + t * 4 * KB)
-                    nc.sync.dma_start(out=r[:], in_=ov[:, t:t + 2, :])
-                    r32[t] = r
-            col_step()
-
         bc = broadcast_bv()
+        bcs = big.tile([P, COLS], F32, name="bcs", offset=OFF_ACC)
+        for h in range(2):
+            nc.scalar.copy(out=bcs[:, h * 512:(h + 1) * 512], in_=bc[h][:])
+        g_pairs = [t for t in range(0, NP, 2) if t < 2 * GPAIRS]
+        v_pairs = [t for t in range(0, NP, 2) if t >= 2 * GPAIRS]
+        for t in g_pairs:
+            for e in range(2):
+                nc.scalar.activation(out=r32[t][:, e, :], in_=r32[t][:, e, :], func=ACT.Copy,
+                                     scale=a_all[:, t + e:t + e + 1])
+        for t in g_pairs:
+            for e in range(2):
+                nc.gpsimd.tensor_tensor(out=r32[t][:, e, :], in0=r32[t][:, e, :], in1=bcs[:],
+                                        op=ALU.mult)
+            nc.scalar.dma_start(out=ov[:, t:t + 2, :], in_=r32[t][:])
         for v in range(NV):
             for h in range(2):
                 hs = slice(h * 512, (h + 1) * 512)
@@ -309,7 +370,7 @@ def tile_differentiablematcher_t_kernel(tc, pred_masks, gt_masks, out):
                     out=ev[v][:, hs], in0=ev[v][:, hs], scalar=a_all[:, NP + v:NP + v + 1],
                     in1=bc[h][:], op0=ALU.mult, op1=ALU.mult)
             nc.sync.dma_start(out=ov[:, NP + v, :], in_=ev[v][:])
-        for t in range(0, NP, 2):
+        for t in v_pairs:
             for e in range(2):
                 for h in range(2):
                     hs = slice(h * 512, (h + 1) * 512)

@@ -26,6 +26,7 @@ INV_TEMP = 10.0
 KB = 1024
 EARLY = 2
 GPAIRS = 5
+REPEAT_IT = 2
 FLOPS = 2 * ROWS * COLS * CONTR
 
 OFF_EAH = 0
@@ -288,14 +289,9 @@ def tile_differentiablematcher_t_kernel(tc, pred_masks, gt_masks, out):
                     in1=acc[:, hs], op0=ALU.mult, op1=ALU.add)
 
         r32 = {}
-        for it in range(ITERS):
-            if it == 0:
-                nc.vector.tensor_reduce(out=s_all[:], in_=rs[:], axis=AX.X, op=ALU.add)
-                nc.vector.reciprocal(out=a_all[:, 0:NP], in_=s_all[:, 0:NP])
-                split(mva, a_all[:, 0:NP])
-                nc.vector.reciprocal(out=a_all[:, NP:RT], in_=s_all[:, NP:RT])
-                early = 0
-            else:
+
+        def row_phase(early):
+            if True:
                 bc = broadcast_bv()
                 rsp = bank(4, [P, NP, NCOL], F32, "rsp")
                 for t in range(NP):
@@ -313,17 +309,13 @@ def tile_differentiablematcher_t_kernel(tc, pred_masks, gt_masks, out):
                             accum_out=svh[:, v, h:h + 1])
                 nc.vector.tensor_reduce(out=s_all[:, NP:RT], in_=svh[:], axis=AX.X, op=ALU.add)
                 nc.vector.reciprocal(out=a_all[:, NP:RT], in_=s_all[:, NP:RT])
-                early = EARLY
                 for i in range(early):
                     acc_step(i // 2, i % 2)
                 nc.vector.tensor_reduce(out=s_all[:, 0:NP], in_=rsp[:, :, 0:2], axis=AX.X, op=ALU.add)
                 nc.vector.reciprocal(out=a_all[:, 0:NP], in_=s_all[:, 0:NP])
                 split(mva, a_all[:, 0:NP])
-            if it == ITERS - 1:
-                for t in range(0, NP, 2):
-                    r = big.tile([P, 2, COLS], F32, name="r32_%d" % t, offset=OFF_EB + t * 4 * KB)
-                    nc.sync.dma_start(out=r[:], in_=ov[:, t:t + 2, :])
-                    r32[t] = r
+
+        def col_phase(early):
             csp = bank(6, [P, CC, 2, NCOL], F32, "csp")
             for jc in range(CC):
                 k = 0
@@ -347,6 +339,26 @@ def tile_differentiablematcher_t_kernel(tc, pred_masks, gt_masks, out):
             nc.vector.tensor_reduce(out=tt[:], in_=csp[:, :, :, 0:2], axis=AX.XY, op=ALU.add)
             nc.vector.reciprocal(out=bv[:], in_=tt[:])
             split(mvb, bv[:])
+
+        for it in range(ITERS):
+            if it == 0:
+                nc.vector.tensor_reduce(out=s_all[:], in_=rs[:], axis=AX.X, op=ALU.add)
+                nc.vector.reciprocal(out=a_all[:, 0:NP], in_=s_all[:, 0:NP])
+                split(mva, a_all[:, 0:NP])
+                nc.vector.reciprocal(out=a_all[:, NP:RT], in_=s_all[:, NP:RT])
+                col_phase(0)
+                continue
+            if it == REPEAT_IT:
+                row_phase(0)
+            row_phase(EARLY)
+            if it == ITERS - 1:
+                for t in range(0, NP, 2):
+                    r = big.tile([P, 2, COLS], F32, name="r32_%d" % t, offset=OFF_EB + t * 4 * KB)
+                    nc.sync.dma_start(out=r[:], in_=ov[:, t:t + 2, :])
+                    r32[t] = r
+            col_phase(EARLY)
+            if it == REPEAT_IT:
+                col_phase(0)
 
         bc = broadcast_bv()
         bcs = big.tile([P, COLS], F32, name="bcs", offset=OFF_ACC)

@@ -26,7 +26,7 @@ INV_TEMP = 10.0
 KB = 1024
 EARLY = 2
 GPAIRS = 5
-REPEAT_IT = 2
+REPEAT_IT = -1
 FLOPS = 2 * ROWS * COLS * CONTR
 
 OFF_EAH = 0
@@ -44,7 +44,7 @@ OFF_ACCL = OFF_MISC + 6 * KB
 OFF_JUNK = OFF_MISC + 8 * KB
 OFF_GRP = OFF_MISC + 10 * KB
 OFF_COD = OFF_MISC + 14 * KB
-OFF_PLN = OFF_MISC + 16 * KB
+OFF_PLN = OFF_MISC + 17 * KB
 
 
 def tile_differentiablematcher_t_kernel(tc, pred_masks, gt_masks, out):
@@ -130,62 +130,66 @@ def tile_differentiablematcher_t_kernel(tc, pred_masks, gt_masks, out):
         ebl = {}
         ev = {}
 
-        def do_transposes(t):
+        tp_of = {}
+
+        def do_transposes(t, g):
             src = p_raw[t // 2][:, t % 2, :].bitcast(F32)
-            tp = bank(t % 2, [P, 2, 2, P], F32, "tp")
-            for g in range(2):
-                for u in range(2):
-                    lo = 256 * g + 128 * u
-                    nc.tensor.transpose(tp[:, g, u, :], src[:, lo:lo + P], ident_f[:])
+            if g == 0:
+                tp_of[t] = bank(t % 2, [P, 2, 2, P], F32, "tp")
+            for u in range(2):
+                lo = 256 * g + 128 * u
+                nc.tensor.transpose(tp_of[t][:, g, u, :], src[:, lo:lo + P], ident_f[:])
+
+        def do_regroup(t):
             grp = big.tile([P, 4 * 256], BF16, name="grp%d" % (t % 2),
                            offset=OFF_GRP + (t % 2) * 2 * KB, align_bytes=64)
             nc.scalar.copy(
                 out=grp[:].bitcast(F32).rearrange("p (g i u) -> p g i u", g=2, u=2),
-                in_=tp[:].rearrange("p g u i -> p g i u"),
+                in_=tp_of[t][:].rearrange("p g u i -> p g i u"),
             )
             grp_of[t] = grp
 
         def do_quantise(t):
-            cod = big.tile([P, 256], U32, name="cod%d" % (t % 2),
-                           offset=OFF_COD + (t % 2) * KB, align_bytes=64)
-            pln = big.tile([P, 256], U8, name="pln%d" % (t % 2),
-                           offset=OFF_PLN + (t % 2) * 256, align_bytes=64)
+            cod = big.tile([P, 256], U32, name="cod%d" % (t % 3),
+                           offset=OFF_COD + (t % 3) * KB, align_bytes=64)
+            pln = big.tile([P, 256], U8, name="pln%d" % (t % 3),
+                           offset=OFF_PLN + (t % 3) * 256, align_bytes=64)
             nc.vector.quantize_mx(out=cod[:].bitcast(FP8X4), scales=pln[:], in_=grp_of[t][:])
             cod_of[t] = (cod, pln)
 
-        def do_mx(t):
+        def do_mx(t, h):
             cod, pln = cod_of[t]
-            ds = []
-            for h in range(2):
-                d = bank(2 + 2 * (t % 2) + h, [P, 512], F32, "d")
-                for g in range(2):
-                    nc.tensor.matmul_mx(
-                        out=d[:],
-                        lhsT=cod[:, g * P:(g + 1) * P].bitcast(FP8X4),
-                        lhsT_scale=pln[:, g * P:(g + 1) * P],
-                        rhs=gc[:, g, h * 512:(h + 1) * 512].bitcast(FP8X4),
-                        rhs_scale=gs[:, g, h * 512:(h + 1) * 512],
-                        start=(g == 0),
-                        stop=(g == 1),
-                    )
-                ds.append(d)
-            d_of[t] = ds
+            d = bank(2 + 2 * (t % 2) + h, [P, 512], F32, "d")
+            for g in range(2):
+                nc.tensor.matmul_mx(
+                    out=d[:],
+                    lhsT=cod[:, g * P:(g + 1) * P].bitcast(FP8X4),
+                    lhsT_scale=pln[:, g * P:(g + 1) * P],
+                    rhs=gc[:, g, h * 512:(h + 1) * 512].bitcast(FP8X4),
+                    rhs_scale=gs[:, g, h * 512:(h + 1) * 512],
+                    start=(g == 0),
+                    stop=(g == 1),
+                )
+            d_of[(t, h)] = d
 
-        def do_max(t):
-            ds = d_of[t]
-            m2 = tiny.tile([P, 2], F32, name="m2")
-            for h in range(2):
-                nc.vector.tensor_reduce(out=m2[:, h:h + 1], in_=ds[h][:], axis=AX.X, op=ALU.max)
-            nb = tiny.tile([P, 1], F32, name="nb")
-            nc.vector.tensor_scalar(out=nb[:], in0=m2[:, 0:1], scalar1=m2[:, 1:2],
-                                    scalar2=-INV_TEMP, op0=ALU.max, op1=ALU.mult)
-            nb_of[t] = nb
+        m2_of = {}
+
+        def do_max(t, h):
+            if h == 0:
+                m2_of[t] = tiny.tile([P, 2], F32, name="m2")
+            m2 = m2_of[t]
+            nc.vector.tensor_reduce(out=m2[:, h:h + 1], in_=d_of[(t, h)][:], axis=AX.X, op=ALU.max)
+            if h == 1:
+                nb = tiny.tile([P, 1], F32, name="nb")
+                nc.vector.tensor_scalar(out=nb[:], in0=m2[:, 0:1], scalar1=m2[:, 1:2],
+                                        scalar2=-INV_TEMP, op0=ALU.max, op1=ALU.mult)
+                nb_of[t] = nb
 
         def do_exp(t):
-            ds = d_of[t]
+            ds = [d_of[(t, 0)], d_of[(t, 1)]]
             if t < NP:
                 dest = big.tile([P, COLS], F32, name="e32_%d" % (t % 3),
-                                offset=OFF_EV + (t % 3) * 8 * KB)
+                                offset=OFF_EV + (4 + 2 * (t % 3)) * 4 * KB)
                 e32_of[t] = dest
             else:
                 dest = big.tile([P, COLS], F32, name="ev%d" % (t - NP),
@@ -209,24 +213,21 @@ def tile_differentiablematcher_t_kernel(tc, pred_masks, gt_masks, out):
             eng.tensor_tensor(out=lo[:], in0=e32_of[t][:], in1=eah[t][:], op=ALU.subtract)
             eal[t] = lo
 
-        def do_eb_transposes(t):
-            pair = []
-            for part in range(2):
-                src = eah[t] if part == 0 else eal[t]
-                ebp = bank(6 + part, [P, CC, P], BF16, "ebp")
-                for jc in range(CC):
-                    nc.tensor.transpose(ebp[:, jc, :], src[:, jc * P:(jc + 1) * P], ident_b[:])
-                pair.append(ebp)
-            ebp_of[t] = pair
+        def do_eb_transposes(t, part):
+            src = eah[t] if part == 0 else eal[t]
+            ebp = bank(6 + part, [P, CC, P], BF16, "ebp")
+            for jc in range(CC):
+                nc.tensor.transpose(ebp[:, jc, :], src[:, jc * P:(jc + 1) * P], ident_b[:])
+            ebp_of[(t, part)] = ebp
 
         def do_eb_copy(t):
             for part in range(2):
                 eb = big.tile([P, CC, P], BF16, name="eb%d_%d" % (part, t),
                               offset=OFF_EB + t * 4 * KB + part * 2 * KB)
-                if part == 1 and t % 2 == 0:
-                    nc.vector.tensor_copy(out=eb[:], in_=ebp_of[t][part][:])
+                if part == 1 and sub_on_gpsimd(t + 2):
+                    nc.vector.tensor_copy(out=eb[:], in_=ebp_of[(t, part)][:])
                 else:
-                    nc.scalar.copy(out=eb[:], in_=ebp_of[t][part][:])
+                    nc.scalar.copy(out=eb[:], in_=ebp_of[(t, part)][:])
                 if part == 0:
                     ebh[t] = eb
                 else:
@@ -235,25 +236,30 @@ def tile_differentiablematcher_t_kernel(tc, pred_masks, gt_masks, out):
         def sub_on_gpsimd(t):
             return t % 3 == 1
 
-        for s in range(-2, RT + 4):
-            if 0 <= s - 2 < NP and not sub_on_gpsimd(s - 2):
-                do_sub(s - 2, nc.vector)
+        for s in range(-3, RT + 6):
+            if 0 <= s + 1 < RT:
+                do_quantise(s + 1)
+            if 0 <= s + 2 < RT:
+                do_regroup(s + 2)
+            if 0 <= s - 5 < NP:
+                do_eb_copy(s - 5)
             if 0 <= s - 1 < RT:
                 do_exp(s - 1)
             if 0 <= s - 1 < NP:
                 do_cast(s - 1)
                 if sub_on_gpsimd(s - 1):
                     do_sub(s - 1, nc.gpsimd)
-            if 0 <= s < RT:
-                do_mx(s)
-                do_max(s)
-            if 0 <= s - 3 < NP:
-                do_eb_transposes(s - 3)
-                do_eb_copy(s - 3)
-            if 0 <= s + 1 < RT:
-                do_quantise(s + 1)
-            if 0 <= s + 2 < RT:
-                do_transposes(s + 2)
+            for h in range(2):
+                if 0 <= s < RT:
+                    do_mx(s, h)
+                if 0 <= s - 4 < NP:
+                    do_eb_transposes(s - 4, h)
+                if 0 <= s + 3 < RT:
+                    do_transposes(s + 3, h)
+                if 0 <= s < RT:
+                    do_max(s, h)
+                if h == 0 and 0 <= s - 3 < NP and not sub_on_gpsimd(s - 3):
+                    do_sub(s - 3, nc.vector)
 
         acc = big.tile([P, COLS], F32, name="acc", offset=OFF_ACC)
         acch = big.tile([P, COLS], BF16, name="acch", offset=OFF_ACCH)

@@ -26,7 +26,10 @@ INV_TEMP = 10.0
 KB = 1024
 EARLY = 2
 GPAIRS = 5
-REPEAT_IT = -1
+GT = NP // 2
+REBUILT = 8
+MID = 13
+COL_SLOTS = {27: [0], 28: [1], 29: [2], 30: [3], 31: [4], 32: [5, 6], 33: [7]}
 FLOPS = 2 * ROWS * COLS * CONTR
 
 OFF_EAH = 0
@@ -38,13 +41,14 @@ OFF_GRAW = OFF_EAH + (NP - 8) * 2 * KB
 OFF_GGRP = OFF_EAL + (NP - 8) * 2 * KB
 OFF_GC = OFF_MISC
 OFF_GS = OFF_MISC + 8 * KB
-OFF_ACC = OFF_MISC
-OFF_ACCH = OFF_MISC + 4 * KB
-OFF_ACCL = OFF_MISC + 6 * KB
-OFF_JUNK = OFF_MISC + 8 * KB
+OFF_ACCH = OFF_MISC
+OFF_ACCL = OFF_MISC + 2 * KB
+OFF_JUNK = OFF_MISC + 4 * KB
+OFF_BCS = OFF_MISC + 6 * KB
 OFF_GRP = OFF_MISC + 10 * KB
 OFF_COD = OFF_MISC + 14 * KB
 OFF_PLN = OFF_MISC + 17 * KB
+OFF_ACC = OFF_PLN + 3 * 256
 
 
 def tile_differentiablematcher_t_kernel(tc, pred_masks, gt_masks, out):
@@ -140,13 +144,15 @@ def tile_differentiablematcher_t_kernel(tc, pred_masks, gt_masks, out):
                 lo = 256 * g + 128 * u
                 nc.tensor.transpose(tp_of[t][:, g, u, :], src[:, lo:lo + P], ident_f[:])
 
-        def do_regroup(t):
+        def do_regroup(t, on_vector):
             grp = big.tile([P, 4 * 256], BF16, name="grp%d" % (t % 2),
                            offset=OFF_GRP + (t % 2) * 2 * KB, align_bytes=64)
-            nc.scalar.copy(
-                out=grp[:].bitcast(F32).rearrange("p (g i u) -> p g i u", g=2, u=2),
-                in_=tp_of[t][:].rearrange("p g u i -> p g i u"),
-            )
+            dst = grp[:].bitcast(F32).rearrange("p (g i u) -> p g i u", g=2, u=2)
+            words = tp_of[t][:].rearrange("p g u i -> p g i u")
+            if on_vector:
+                nc.vector.tensor_copy(out=dst, in_=words)
+            else:
+                nc.scalar.copy(out=dst, in_=words)
             grp_of[t] = grp
 
         def do_quantise(t):
@@ -195,22 +201,25 @@ def tile_differentiablematcher_t_kernel(tc, pred_masks, gt_masks, out):
                 dest = big.tile([P, COLS], F32, name="ev%d" % (t - NP),
                                 offset=OFF_EV + (t - NP) * 4 * KB)
                 ev[t - NP] = dest
+            if t < NP:
+                eah[t] = big.tile([P, COLS], BF16, name="eah%d" % t, offset=OFF_EAH + t * 2 * KB)
             for h in range(2):
-                nc.scalar.activation(out=dest[:, h * 512:(h + 1) * 512], in_=ds[h][:], func=ACT.Exp,
+                hs = slice(h * 512, (h + 1) * 512)
+                nc.scalar.activation(out=dest[:, hs], in_=ds[h][:], func=ACT.Exp,
                                      bias=nb_of[t][:, 0:1], scale=INV_TEMP,
                                      accum_out=rs[:, t, h:h + 1])
-            if t < NP:
+                if t < NP:
+                    nc.scalar.activation(out=eah[t][:, hs], in_=ds[h][:], func=ACT.Exp,
+                                         bias=nb_of[t][:, 0:1], scale=INV_TEMP)
+            if t < NP - REBUILT:
                 nc.sync.dma_start(out=ov[:, t, :], in_=dest[:])
 
-        def do_cast(t):
-            hi = big.tile([P, COLS], BF16, name="eah%d" % t, offset=OFF_EAH + t * 2 * KB)
-            nc.gpsimd.tensor_scalar(out=hi[:], in0=e32_of[t][:], scalar1=1.0, scalar2=0.0,
-                                    op0=ALU.mult, op1=ALU.add)
-            eah[t] = hi
-
-        def do_sub(t, eng):
+        def do_sub(t):
             lo = big.tile([P, COLS], BF16, name="eal%d" % t, offset=OFF_EAL + t * 2 * KB)
-            eng.tensor_tensor(out=lo[:], in0=e32_of[t][:], in1=eah[t][:], op=ALU.subtract)
+            for h in range(2):
+                hs = slice(h * 512, (h + 1) * 512)
+                nc.gpsimd.tensor_tensor(out=lo[:, hs], in0=e32_of[t][:, hs], in1=eah[t][:, hs],
+                                        op=ALU.subtract)
             eal[t] = lo
 
         def do_eb_transposes(t, part):
@@ -220,11 +229,11 @@ def tile_differentiablematcher_t_kernel(tc, pred_masks, gt_masks, out):
                 nc.tensor.transpose(ebp[:, jc, :], src[:, jc * P:(jc + 1) * P], ident_b[:])
             ebp_of[(t, part)] = ebp
 
-        def do_eb_copy(t):
+        def do_eb_copy(t, lo_on_vector):
             for part in range(2):
                 eb = big.tile([P, CC, P], BF16, name="eb%d_%d" % (part, t),
                               offset=OFF_EB + t * 4 * KB + part * 2 * KB)
-                if part == 1 and sub_on_gpsimd(t + 2):
+                if part == 1 and lo_on_vector:
                     nc.vector.tensor_copy(out=eb[:], in_=ebp_of[(t, part)][:])
                 else:
                     nc.scalar.copy(out=eb[:], in_=ebp_of[(t, part)][:])
@@ -233,56 +242,18 @@ def tile_differentiablematcher_t_kernel(tc, pred_masks, gt_masks, out):
                 else:
                     ebl[t] = eb
 
-        def sub_on_gpsimd(t):
-            return t % 3 == 1
-
-        for s in range(-3, RT + 6):
-            if 0 <= s + 1 < RT:
-                do_quantise(s + 1)
-            if 0 <= s + 2 < RT:
-                do_regroup(s + 2)
-            if 0 <= s - 5 < NP:
-                do_eb_copy(s - 5)
-            if 0 <= s - 1 < RT:
-                do_exp(s - 1)
-            if 0 <= s - 1 < NP:
-                do_cast(s - 1)
-                if sub_on_gpsimd(s - 1):
-                    do_sub(s - 1, nc.gpsimd)
-            for h in range(2):
-                if 0 <= s < RT:
-                    do_mx(s, h)
-                if 0 <= s - 4 < NP:
-                    do_eb_transposes(s - 4, h)
-                if 0 <= s + 3 < RT:
-                    do_transposes(s + 3, h)
-                if 0 <= s < RT:
-                    do_max(s, h)
-                if h == 0 and 0 <= s - 3 < NP and not sub_on_gpsimd(s - 3):
-                    do_sub(s - 3, nc.vector)
-
         acc = big.tile([P, COLS], F32, name="acc", offset=OFF_ACC)
-        acch = big.tile([P, COLS], BF16, name="acch", offset=OFF_ACCH)
-        accl = big.tile([P, COLS], BF16, name="accl", offset=OFF_ACCL)
-        junk = big.tile([P, 512], F32, name="junk", offset=OFF_JUNK)
+        csp_of = {}
 
         def split(mv, vec):
             nc.vector.tensor_copy(out=mv[:, :, 0:1], in_=vec.unsqueeze(2))
             nc.vector.tensor_tensor(out=mv[:, :, 1:2], in0=vec.unsqueeze(2), in1=mv[:, :, 0:1],
                                     op=ALU.subtract)
 
-        def broadcast_bv():
-            bc = []
-            for h in range(2):
-                b = bank(2 + h, [P, 512], F32, "bc")
-                bc.append(b)
-            for jc in range(CC):
-                o = bc[jc // 4][:, (jc % 4) * P:(jc % 4 + 1) * P]
-                nc.tensor.matmul(o, lhsT=mvb[:, jc, 0:1].to_broadcast([P, P]), rhs=ident_b[:],
-                                 start=True, stop=False)
-                nc.tensor.matmul(o, lhsT=mvb[:, jc, 1:2].to_broadcast([P, P]), rhs=ident_b[:],
-                                 start=False, stop=True)
-            return bc
+        def a_of_p_tiles(lo, hi, sums):
+            nc.vector.tensor_reduce(out=s_all[:, lo:hi], in_=sums, axis=AX.X, op=ALU.add)
+            nc.vector.reciprocal(out=a_all[:, lo:hi], in_=s_all[:, lo:hi])
+            split(mva[:, lo:hi, :], a_all[:, lo:hi])
 
         def acc_step(v, h):
             hs = slice(h * 512, (h + 1) * 512)
@@ -294,84 +265,155 @@ def tile_differentiablematcher_t_kernel(tc, pred_masks, gt_masks, out):
                     out=acc[:, hs], in0=ev[v][:, hs], scalar=a_all[:, NP + v:NP + v + 1],
                     in1=acc[:, hs], op0=ALU.mult, op1=ALU.add)
 
-        r32 = {}
+        def col_open():
+            csp_of[0] = bank(6, [P, CC, 3, NCOL], F32, "csp")
 
-        def row_phase(early):
-            if True:
-                bc = broadcast_bv()
-                rsp = bank(4, [P, NP, NCOL], F32, "rsp")
-                for t in range(NP):
-                    k = 0
-                    for jc in range(CC):
-                        for eb in (ebh[t], ebl[t]):
-                            nc.tensor.matmul(rsp[:, t, :], lhsT=eb[:, jc, :], rhs=mvb[:, jc, :],
-                                             start=(k == 0), stop=(k == 2 * CC - 1))
-                            k += 1
-                for v in range(NV):
-                    for h in range(2):
-                        nc.vector.scalar_tensor_tensor(
-                            out=junk[:], in0=ev[v][:, h * 512:(h + 1) * 512], scalar=1.0,
-                            in1=bc[h][:], op0=ALU.mult, op1=ALU.mult,
-                            accum_out=svh[:, v, h:h + 1])
-                nc.vector.tensor_reduce(out=s_all[:, NP:RT], in_=svh[:], axis=AX.X, op=ALU.add)
-                nc.vector.reciprocal(out=a_all[:, NP:RT], in_=s_all[:, NP:RT])
-                for i in range(early):
-                    acc_step(i // 2, i % 2)
-                nc.vector.tensor_reduce(out=s_all[:, 0:NP], in_=rsp[:, :, 0:2], axis=AX.X, op=ALU.add)
-                nc.vector.reciprocal(out=a_all[:, 0:NP], in_=s_all[:, 0:NP])
-                split(mva, a_all[:, 0:NP])
+        def col_pe(jc, g):
+            k = 0
+            for t in range(g * GT, (g + 1) * GT):
+                for ea in (eah[t], eal[t]):
+                    nc.tensor.matmul(csp_of[0][:, jc, g, :], lhsT=ea[:, jc * P:(jc + 1) * P],
+                                     rhs=mva[:, t, :], start=(k == 0), stop=(k == 2 * GT - 1))
+                    k += 1
 
-        def col_phase(early):
-            csp = bank(6, [P, CC, 2, NCOL], F32, "csp")
+        for s in range(-3, RT + 2):
+            scalar_full = s <= NP
+            if 0 <= s + 1 < RT:
+                do_quantise(s + 1)
+            if 0 <= s + 2 < RT:
+                do_regroup(s + 2, scalar_full)
+            if s == NP + 1:
+                a_of_p_tiles(0, NP, rs[:, 0:NP, :])
+            if 0 <= s - 1 < RT:
+                do_exp(s - 1)
+            if 0 <= s - 2 < NP:
+                do_sub(s - 2)
+            if NP <= s - 2 < RT:
+                t = s - 2
+                nc.vector.tensor_reduce(out=s_all[:, t:t + 1], in_=rs[:, t, :], axis=AX.X, op=ALU.add)
+                nc.vector.reciprocal(out=a_all[:, t:t + 1], in_=s_all[:, t:t + 1])
+                acc_step(t - NP, 0)
+                acc_step(t - NP, 1)
+            for h in range(2):
+                if 0 <= s < RT:
+                    do_mx(s, h)
+                if 0 <= s - 4 < NP:
+                    do_eb_transposes(s - 4, h)
+                if 0 <= s + 3 < RT:
+                    do_transposes(s + 3, h)
+                if 0 <= s < RT:
+                    do_max(s, h)
+            if 0 <= s - 4 < NP:
+                do_eb_copy(s - 4, scalar_full)
+            for jc in COL_SLOTS.get(s, []):
+                if jc == 0:
+                    col_open()
+                col_pe(jc, 0)
+                col_pe(jc, 1)
+
+        acch = big.tile([P, COLS], BF16, name="acch", offset=OFF_ACCH)
+        accl = big.tile([P, COLS], BF16, name="accl", offset=OFF_ACCL)
+        junk = big.tile([P, 512], F32, name="junk", offset=OFF_JUNK)
+
+        def broadcast_bv():
+            bc = []
+            for h in range(2):
+                b = bank(2 + h, [P, 512], F32, "bc")
+                bc.append(b)
             for jc in range(CC):
-                k = 0
-                for t in range(NP):
-                    for ea in (eah[t], eal[t]):
-                        nc.tensor.matmul(csp[:, jc, 0, :], lhsT=ea[:, jc * P:(jc + 1) * P],
-                                         rhs=mva[:, t, :], start=(k == 0), stop=(k == 2 * NP - 1))
-                        k += 1
-            for i in range(early, 2 * NV):
+                o = bc[jc // 4][:, (jc % 4) * P:(jc % 4 + 1) * P]
+                nc.tensor.transpose(o, bv[:, jc:jc + 1].to_broadcast([P, P]), ident_f[:])
+            return bc
+
+        def col_finish(first_left):
+            csp = csp_of[0]
+            for i in range(first_left, 2 * NV):
                 acc_step(i // 2, i % 2)
+                if i >= 2 * NV - 2:
+                    hs = slice((i % 2) * 512, (i % 2 + 1) * 512)
+                    nc.scalar.copy(out=acch[:, hs], in_=acc[:, hs])
+            if first_left >= 2 * NV:
+                for h in range(2):
+                    nc.scalar.copy(out=acch[:, h * 512:(h + 1) * 512], in_=acc[:, h * 512:(h + 1) * 512])
             for h in range(2):
                 hs = slice(h * 512, (h + 1) * 512)
-                nc.vector.tensor_copy(out=acch[:, hs], in_=acc[:, hs])
                 nc.vector.tensor_tensor(out=accl[:, hs], in0=acc[:, hs], in1=acch[:, hs],
                                         op=ALU.subtract)
                 for jc in range(4 * h, 4 * h + 4):
-                    nc.tensor.matmul(csp[:, jc, 1, :], lhsT=acch[:, jc * P:(jc + 1) * P],
+                    nc.tensor.matmul(csp[:, jc, 2, :], lhsT=acch[:, jc * P:(jc + 1) * P],
                                      rhs=onescol[:], start=True, stop=False)
-                    nc.tensor.matmul(csp[:, jc, 1, :], lhsT=accl[:, jc * P:(jc + 1) * P],
+                    nc.tensor.matmul(csp[:, jc, 2, :], lhsT=accl[:, jc * P:(jc + 1) * P],
                                      rhs=onescol[:], start=False, stop=True)
-            nc.vector.tensor_reduce(out=tt[:], in_=csp[:, :, :, 0:2], axis=AX.XY, op=ALU.add)
+            nc.vector.tensor_reduce(out=tt[:], in_=csp[:], axis=AX.XY, op=ALU.add)
             nc.vector.reciprocal(out=bv[:], in_=tt[:])
             split(mvb, bv[:])
 
-        for it in range(ITERS):
-            if it == 0:
-                nc.vector.tensor_reduce(out=s_all[:], in_=rs[:], axis=AX.X, op=ALU.add)
-                nc.vector.reciprocal(out=a_all[:, 0:NP], in_=s_all[:, 0:NP])
-                split(mva, a_all[:, 0:NP])
-                nc.vector.reciprocal(out=a_all[:, NP:RT], in_=s_all[:, NP:RT])
-                col_phase(0)
-                continue
-            if it == REPEAT_IT:
-                row_phase(0)
-            row_phase(EARLY)
+        def row_phase():
+            bc = broadcast_bv()
+            rsp = [bank(4 + g, [P, GT, NCOL], F32, "rsp") for g in range(2)]
+            for t in range(NP):
+                k = 0
+                for jc in range(CC):
+                    for eb in (ebh[t], ebl[t]):
+                        nc.tensor.matmul(rsp[t // GT][:, t % GT, :], lhsT=eb[:, jc, :],
+                                         rhs=mvb[:, jc, :],
+                                         start=(k == 0), stop=(k == 2 * CC - 1))
+                        k += 1
+            for i in range(2 * NV):
+                v = i // 2
+                h = i % 2
+                nc.vector.scalar_tensor_tensor(
+                    out=junk[:], in0=ev[v][:, h * 512:(h + 1) * 512], scalar=1.0,
+                    in1=bc[h][:], op0=ALU.mult, op1=ALU.mult,
+                    accum_out=svh[:, v, h:h + 1])
+                if i == MID - 1:
+                    a_of_p_tiles(0, GT, rsp[0][:])
+            nc.vector.tensor_reduce(out=s_all[:, NP:RT], in_=svh[:], axis=AX.X, op=ALU.add)
+            nc.vector.reciprocal(out=a_all[:, NP:RT], in_=s_all[:, NP:RT])
+            for i in range(EARLY):
+                acc_step(i // 2, i % 2)
+            a_of_p_tiles(GT, NP, rsp[1][:])
+
+        def col_phase():
+            col_open()
+            for g in range(2):
+                for jc in range(CC):
+                    col_pe(jc, g)
+            col_finish(EARLY)
+
+        r32 = {}
+        col_finish(2 * NV)
+        for it in range(1, ITERS):
+            row_phase()
             if it == ITERS - 1:
                 for t in range(0, NP, 2):
                     r = big.tile([P, 2, COLS], F32, name="r32_%d" % t, offset=OFF_EB + t * 4 * KB)
-                    nc.sync.dma_start(out=r[:], in_=ov[:, t:t + 2, :])
+                    if t < NP - REBUILT:
+                        nc.sync.dma_start(out=r[:], in_=ov[:, t:t + 2, :])
                     r32[t] = r
-            col_phase(EARLY)
-            if it == REPEAT_IT:
-                col_phase(0)
+            col_phase()
 
         bc = broadcast_bv()
-        bcs = big.tile([P, COLS], F32, name="bcs", offset=OFF_ACC)
+        bcs = big.tile([P, COLS], F32, name="bcs", offset=OFF_BCS)
         for h in range(2):
             nc.scalar.copy(out=bcs[:, h * 512:(h + 1) * 512], in_=bc[h][:])
         g_pairs = [t for t in range(0, NP, 2) if t < 2 * GPAIRS]
-        v_pairs = [t for t in range(0, NP, 2) if t >= 2 * GPAIRS]
+        v_pairs = [t for t in range(0, NP - REBUILT, 2) if t >= 2 * GPAIRS]
+        r_tiles = list(range(NP - REBUILT, NP))
+        sum_banks = [(0, 1), (4, 5), (6, 7)]
+        sums = {}
+
+        def rebuild(i):
+            t = r_tiles[i]
+            for h in range(2):
+                hs = slice(h * 512, (h + 1) * 512)
+                esum = bank(sum_banks[i % 3][h], [P, 512], F32, "esum")
+                nc.tensor.matmul(esum[:], lhsT=ident_b[:], rhs=eah[t][:, hs], start=True, stop=False)
+                nc.tensor.matmul(esum[:], lhsT=ident_b[:], rhs=eal[t][:, hs], start=False, stop=True)
+                sums[(t, h)] = esum
+
+        for i in range(3):
+            rebuild(i)
         for t in g_pairs:
             for e in range(2):
                 nc.scalar.activation(out=r32[t][:, e, :], in_=r32[t][:, e, :], func=ACT.Copy,
@@ -388,6 +430,16 @@ def tile_differentiablematcher_t_kernel(tc, pred_masks, gt_masks, out):
                     out=ev[v][:, hs], in0=ev[v][:, hs], scalar=a_all[:, NP + v:NP + v + 1],
                     in1=bc[h][:], op0=ALU.mult, op1=ALU.mult)
             nc.sync.dma_start(out=ov[:, NP + v, :], in_=ev[v][:])
+        for i, t in enumerate(r_tiles):
+            for h in range(2):
+                hs = slice(h * 512, (h + 1) * 512)
+                nc.vector.scalar_tensor_tensor(
+                    out=r32[t - t % 2][:, t % 2, hs], in0=sums[(t, h)][:],
+                    scalar=a_all[:, t:t + 1], in1=bcs[:, hs], op0=ALU.mult, op1=ALU.mult)
+            if i + 3 < REBUILT:
+                rebuild(i + 3)
+            if t % 2 == 1:
+                nc.sync.dma_start(out=ov[:, t - 1:t + 1, :], in_=r32[t - 1][:])
         for t in v_pairs:
             for e in range(2):
                 for h in range(2):

@@ -29,7 +29,7 @@ GPAIRS = 5
 GT = NP // 2
 REBUILT = 8
 MID = 13
-COL_SLOTS = {27: [0], 28: [1], 29: [2], 30: [3], 31: [4], 32: [5, 6], 33: [7]}
+COL_SLOTS = {26: [0], 27: [1], 28: [2], 29: [3], 30: [4], 31: [5], 32: [6, 7]}
 FLOPS = 2 * ROWS * COLS * CONTR
 
 OFF_EAH = 0
@@ -278,8 +278,6 @@ def tile_differentiablematcher_t_kernel(tc, pred_masks, gt_masks, out):
 
         for s in range(-3, RT + 2):
             scalar_full = s <= NP
-            if 0 <= s + 1 < RT:
-                do_quantise(s + 1)
             if 0 <= s + 2 < RT:
                 do_regroup(s + 2, scalar_full)
             if s == NP + 1:
@@ -297,12 +295,17 @@ def tile_differentiablematcher_t_kernel(tc, pred_masks, gt_masks, out):
             for h in range(2):
                 if 0 <= s < RT:
                     do_mx(s, h)
+            for h in range(2):
                 if 0 <= s - 4 < NP:
                     do_eb_transposes(s - 4, h)
+            for h in range(2):
                 if 0 <= s + 3 < RT:
                     do_transposes(s + 3, h)
+            for h in range(2):
                 if 0 <= s < RT:
                     do_max(s, h)
+            if 0 <= s + 2 < RT:
+                do_quantise(s + 2)
             if 0 <= s - 4 < NP:
                 do_eb_copy(s - 4, scalar_full)
             for jc in COL_SLOTS.get(s, []):

from contextlib import ExitStack

import concourse.mybir as mybir
from concourse.masks import make_identity

F32 = mybir.dt.float32
BF16 = mybir.dt.bfloat16
U32 = mybir.dt.uint32
U8 = mybir.dt.uint8
FP8X4 = mybir.dt.float8_e4m3fn_x4
ALU = mybir.AluOpType
ACT = mybir.ActivationFunctionType
AX = mybir.AxisListType

P = 128
ROWS = 4096
COLS = 1024
CONTR = 1024
RT = ROWS // P
CC = COLS // P
NP = 22
NV = RT - NP
NCOL = 2
ITERS = 5
INV_TEMP = 10.0
KB = 1024
EARLY = 2
GPAIRS = 5
GT = NP // 2
REBUILT = 8
MID = 13
COL_SLOTS = {26: [0], 27: [1], 28: [2], 29: [3], 30: [4], 31: [5], 32: [6, 7]}
FLOPS = 2 * ROWS * COLS * CONTR

OFF_EAH = 0
OFF_EAL = OFF_EAH + NP * 2 * KB
OFF_EB = OFF_EAL + NP * 2 * KB
OFF_EV = OFF_EB + NP * 4 * KB
OFF_MISC = OFF_EV + NV * 4 * KB
OFF_GRAW = OFF_EAH + (NP - 8) * 2 * KB
OFF_GGRP = OFF_EAL + (NP - 8) * 2 * KB
OFF_GC = OFF_MISC
OFF_GS = OFF_MISC + 8 * KB
OFF_ACCH = OFF_MISC
OFF_ACCL = OFF_MISC + 2 * KB
OFF_JUNK = OFF_MISC + 4 * KB
OFF_BCS = OFF_MISC + 6 * KB
OFF_GRP = OFF_MISC + 10 * KB
OFF_COD = OFF_MISC + 14 * KB
OFF_PLN = OFF_MISC + 17 * KB
OFF_ACC = OFF_PLN + 3 * 256


def tile_differentiablematcher_t_kernel(tc, pred_masks, gt_masks, out):
    nc = tc.nc
    pv = pred_masks.rearrange("b (p t) h w -> (b p) t (h w)", t=RT)
    gv = gt_masks.rearrange("(c p) h w -> p c (h w)", p=P)
    ov = out.rearrange("b (p t) n -> (b p) t n", t=RT)

    with ExitStack() as ctx:
        big = ctx.enter_context(tc.tile_pool(name="big", bufs=1))
        small = ctx.enter_context(tc.tile_pool(name="small", bufs=1))
        tiny = ctx.enter_context(tc.tile_pool(name="tiny", bufs=4))
        ps = ctx.enter_context(tc.psum_pool(name="ps", bufs=1))
        ctx.enter_context(tc.manual_schedule())

        def bank(b, shape, dtype, name):
            return ps.tile(shape, dtype, name=name, tag="bk%d" % b)

        g_raw = big.tile([P, CC, CONTR], BF16, name="g_raw", offset=OFF_GRAW)
        for q in range(4):
            nc.sync.dma_start(out=g_raw[:, 2 * q:2 * q + 2, :], in_=gv[:, 2 * q:2 * q + 2, :])
        p_raw = []
        for n in range(RT // 2):
            if 2 * n < NP:
                off = OFF_EB + 2 * n * 4 * KB
            else:
                off = OFF_EV + (2 * n - NP + 1) * 4 * KB
            r = big.tile([P, 2, CONTR], BF16, name="p_raw%d" % n, offset=off)
            nc.sync.dma_start(out=r[:], in_=pv[:, 2 * n:2 * n + 2, :])
            p_raw.append(r)

        ident_f = small.tile([P, P], F32, name="ident_f")
        make_identity(nc, ident_f[:])
        ident_b = small.tile([P, P], BF16, name="ident_b")
        make_identity(nc, ident_b[:])
        onescol = small.tile([P, NCOL], BF16, name="onescol")
        nc.vector.memset(onescol[:], 0.0)
        nc.vector.memset(onescol[:, 0:1], 1.0)
        mva = small.tile([P, NP, NCOL], BF16, name="mva")
        nc.vector.memset(mva[:], 0.0)
        mvb = small.tile([P, CC, NCOL], BF16, name="mvb")
        nc.vector.memset(mvb[:], 0.0)
        rs = small.tile([P, RT, 2], F32, name="rs")
        s_all = small.tile([P, RT], F32, name="s_all")
        a_all = small.tile([P, RT], F32, name="a_all")
        svh = small.tile([P, NV, 2], F32, name="svh")
        tt = small.tile([P, CC], F32, name="tt")
        bv = small.tile([P, CC], F32, name="bv")

        g_grp = big.tile([P, 2, 4 * COLS], BF16, name="g_grp", offset=OFF_GGRP, align_bytes=64)
        g_grp_w = g_grp[:].bitcast(F32).rearrange("p g (j u) -> p g j u", u=2)
        gc = big.tile([P, 2, COLS], U32, name="gc", offset=OFF_GC, align_bytes=64)
        gs = big.tile([P, 2, COLS], U8, name="gs", offset=OFF_GS, align_bytes=64)
        for half in range(2):
            for jc in range(4 * half, 4 * half + 4):
                tpg = bank(jc, [P, 2, 2, P], F32, "tpg")
                src = g_raw[:, jc, :].bitcast(F32)
                for g in range(2):
                    for u in range(2):
                        lo = 256 * g + 128 * u
                        nc.tensor.transpose(tpg[:, g, u, :], src[:, lo:lo + P], ident_f[:])
                dst = g_grp_w[:, :, jc * P:(jc + 1) * P, :]
                if jc % 2 == 0:
                    nc.vector.tensor_copy(out=dst, in_=tpg[:].rearrange("p g u w -> p g w u"))
                else:
                    nc.scalar.copy(out=dst, in_=tpg[:].rearrange("p g u w -> p g w u"))
            for g in range(2):
                nc.vector.quantize_mx(
                    out=gc[:, g, half * 512:(half + 1) * 512].bitcast(FP8X4),
                    scales=gs[:, g, half * 512:(half + 1) * 512],
                    in_=g_grp[:, g, half * 2048:(half + 1) * 2048],
                )

        grp_of = {}
        cod_of = {}
        d_of = {}
        nb_of = {}
        e32_of = {}
        eah = {}
        eal = {}
        ebp_of = {}
        ebh = {}
        ebl = {}
        ev = {}

        tp_of = {}

        def do_transposes(t, g):
            src = p_raw[t // 2][:, t % 2, :].bitcast(F32)
            if g == 0:
                tp_of[t] = bank(t % 2, [P, 2, 2, P], F32, "tp")
            for u in range(2):
                lo = 256 * g + 128 * u
                nc.tensor.transpose(tp_of[t][:, g, u, :], src[:, lo:lo + P], ident_f[:])

        def do_regroup(t, on_vector):
            grp = big.tile([P, 4 * 256], BF16, name="grp%d" % (t % 2),
                           offset=OFF_GRP + (t % 2) * 2 * KB, align_bytes=64)
            dst = grp[:].bitcast(F32).rearrange("p (g i u) -> p g i u", g=2, u=2)
            words = tp_of[t][:].rearrange("p g u i -> p g i u")
            if on_vector:
                nc.vector.tensor_copy(out=dst, in_=words)
            else:
                nc.scalar.copy(out=dst, in_=words)
            grp_of[t] = grp

        def do_quantise(t):
            cod = big.tile([P, 256], U32, name="cod%d" % (t % 3),
                           offset=OFF_COD + (t % 3) * KB, align_bytes=64)
            pln = big.tile([P, 256], U8, name="pln%d" % (t % 3),
                           offset=OFF_PLN + (t % 3) * 256, align_bytes=64)
            nc.vector.quantize_mx(out=cod[:].bitcast(FP8X4), scales=pln[:], in_=grp_of[t][:])
            cod_of[t] = (cod, pln)

        def do_mx(t, h):
            cod, pln = cod_of[t]
            d = bank(2 + 2 * (t % 2) + h, [P, 512], F32, "d")
            for g in range(2):
                nc.tensor.matmul_mx(
                    out=d[:],
                    lhsT=cod[:, g * P:(g + 1) * P].bitcast(FP8X4),
                    lhsT_scale=pln[:, g * P:(g + 1) * P],
                    rhs=gc[:, g, h * 512:(h + 1) * 512].bitcast(FP8X4),
                    rhs_scale=gs[:, g, h * 512:(h + 1) * 512],
                    start=(g == 0),
                    stop=(g == 1),
                )
            d_of[(t, h)] = d

        m2_of = {}

        def do_max(t, h):
            if h == 0:
                m2_of[t] = tiny.tile([P, 2], F32, name="m2")
            m2 = m2_of[t]
            nc.vector.tensor_reduce(out=m2[:, h:h + 1], in_=d_of[(t, h)][:], axis=AX.X, op=ALU.max)
            if h == 1:
                nb = tiny.tile([P, 1], F32, name="nb")
                nc.vector.tensor_scalar(out=nb[:], in0=m2[:, 0:1], scalar1=m2[:, 1:2],
                                        scalar2=-INV_TEMP, op0=ALU.max, op1=ALU.mult)
                nb_of[t] = nb

        def do_exp(t):
            ds = [d_of[(t, 0)], d_of[(t, 1)]]
            if t < NP:
                dest = big.tile([P, COLS], F32, name="e32_%d" % (t % 3),
                                offset=OFF_EV + (4 + 2 * (t % 3)) * 4 * KB)
                e32_of[t] = dest
            else:
                dest = big.tile([P, COLS], F32, name="ev%d" % (t - NP),
                                offset=OFF_EV + (t - NP) * 4 * KB)
                ev[t - NP] = dest
            if t < NP:
                eah[t] = big.tile([P, COLS], BF16, name="eah%d" % t, offset=OFF_EAH + t * 2 * KB)
            for h in range(2):
                hs = slice(h * 512, (h + 1) * 512)
                nc.scalar.activation(out=dest[:, hs], in_=ds[h][:], func=ACT.Exp,
                                     bias=nb_of[t][:, 0:1], scale=INV_TEMP,
                                     accum_out=rs[:, t, h:h + 1])
                if t < NP:
                    nc.scalar.activation(out=eah[t][:, hs], in_=ds[h][:], func=ACT.Exp,
                                         bias=nb_of[t][:, 0:1], scale=INV_TEMP)
            if t < NP - REBUILT:
                nc.sync.dma_start(out=ov[:, t, :], in_=dest[:])

        def do_sub(t):
            lo = big.tile([P, COLS], BF16, name="eal%d" % t, offset=OFF_EAL + t * 2 * KB)
            for h in range(2):
                hs = slice(h * 512, (h + 1) * 512)
                nc.gpsimd.tensor_tensor(out=lo[:, hs], in0=e32_of[t][:, hs], in1=eah[t][:, hs],
                                        op=ALU.subtract)
            eal[t] = lo

        def do_eb_transposes(t, part):
            src = eah[t] if part == 0 else eal[t]
            ebp = bank(6 + part, [P, CC, P], BF16, "ebp")
            for jc in range(CC):
                nc.tensor.transpose(ebp[:, jc, :], src[:, jc * P:(jc + 1) * P], ident_b[:])
            ebp_of[(t, part)] = ebp

        def do_eb_copy(t, lo_on_vector):
            for part in range(2):
                eb = big.tile([P, CC, P], BF16, name="eb%d_%d" % (part, t),
                              offset=OFF_EB + t * 4 * KB + part * 2 * KB)
                if part == 1 and lo_on_vector:
                    nc.vector.tensor_copy(out=eb[:], in_=ebp_of[(t, part)][:])
                else:
                    nc.scalar.copy(out=eb[:], in_=ebp_of[(t, part)][:])
                if part == 0:
                    ebh[t] = eb
                else:
                    ebl[t] = eb

        acc = big.tile([P, COLS], F32, name="acc", offset=OFF_ACC)
        csp_of = {}

        def split(mv, vec):
            nc.vector.tensor_copy(out=mv[:, :, 0:1], in_=vec.unsqueeze(2))
            nc.vector.tensor_tensor(out=mv[:, :, 1:2], in0=vec.unsqueeze(2), in1=mv[:, :, 0:1],
                                    op=ALU.subtract)

        def a_of_p_tiles(lo, hi, sums):
            nc.vector.tensor_reduce(out=s_all[:, lo:hi], in_=sums, axis=AX.X, op=ALU.add)
            nc.vector.reciprocal(out=a_all[:, lo:hi], in_=s_all[:, lo:hi])
            split(mva[:, lo:hi, :], a_all[:, lo:hi])

        def acc_step(v, h):
            hs = slice(h * 512, (h + 1) * 512)
            if v == 0:
                nc.vector.tensor_scalar(out=acc[:, hs], in0=ev[v][:, hs],
                                        scalar1=a_all[:, NP:NP + 1], scalar2=None, op0=ALU.mult)
            else:
                nc.vector.scalar_tensor_tensor(
                    out=acc[:, hs], in0=ev[v][:, hs], scalar=a_all[:, NP + v:NP + v + 1],
                    in1=acc[:, hs], op0=ALU.mult, op1=ALU.add)

        def col_open():
            csp_of[0] = bank(6, [P, CC, 3, NCOL], F32, "csp")

        def col_pe(jc, g):
            k = 0
            for t in range(g * GT, (g + 1) * GT):
                for ea in (eah[t], eal[t]):
                    nc.tensor.matmul(csp_of[0][:, jc, g, :], lhsT=ea[:, jc * P:(jc + 1) * P],
                                     rhs=mva[:, t, :], start=(k == 0), stop=(k == 2 * GT - 1))
                    k += 1

        for s in range(-3, RT + 2):
            scalar_full = s <= NP
            if 0 <= s + 2 < RT:
                do_regroup(s + 2, scalar_full)
            if s == NP + 1:
                a_of_p_tiles(0, NP, rs[:, 0:NP, :])
            if 0 <= s - 1 < RT:
                do_exp(s - 1)
            if 0 <= s - 2 < NP:
                do_sub(s - 2)
            if NP <= s - 2 < RT:
                t = s - 2
                nc.vector.tensor_reduce(out=s_all[:, t:t + 1], in_=rs[:, t, :], axis=AX.X, op=ALU.add)
                nc.vector.reciprocal(out=a_all[:, t:t + 1], in_=s_all[:, t:t + 1])
                acc_step(t - NP, 0)
                acc_step(t - NP, 1)
            for h in range(2):
                if 0 <= s < RT:
                    do_mx(s, h)
            for h in range(2):
                if 0 <= s - 4 < NP:
                    do_eb_transposes(s - 4, h)
            for h in range(2):
                if 0 <= s + 3 < RT:
                    do_transposes(s + 3, h)
            for h in range(2):
                if 0 <= s < RT:
                    do_max(s, h)
            if 0 <= s + 2 < RT:
                do_quantise(s + 2)
            if 0 <= s - 4 < NP:
                do_eb_copy(s - 4, scalar_full)
            for jc in COL_SLOTS.get(s, []):
                if jc == 0:
                    col_open()
                col_pe(jc, 0)
                col_pe(jc, 1)

        acch = big.tile([P, COLS], BF16, name="acch", offset=OFF_ACCH)
        accl = big.tile([P, COLS], BF16, name="accl", offset=OFF_ACCL)
        junk = big.tile([P, 512], F32, name="junk", offset=OFF_JUNK)

        def broadcast_bv():
            bc = []
            for h in range(2):
                b = bank(2 + h, [P, 512], F32, "bc")
                bc.append(b)
            for jc in range(CC):
                o = bc[jc // 4][:, (jc % 4) * P:(jc % 4 + 1) * P]
                nc.tensor.transpose(o, bv[:, jc:jc + 1].to_broadcast([P, P]), ident_f[:])
            return bc

        def col_finish(first_left):
            csp = csp_of[0]
            for i in range(first_left, 2 * NV):
                acc_step(i // 2, i % 2)
                if i >= 2 * NV - 2:
                    hs = slice((i % 2) * 512, (i % 2 + 1) * 512)
                    nc.scalar.copy(out=acch[:, hs], in_=acc[:, hs])
            if first_left >= 2 * NV:
                for h in range(2):
                    nc.scalar.copy(out=acch[:, h * 512:(h + 1) * 512], in_=acc[:, h * 512:(h + 1) * 512])
            for h in range(2):
                hs = slice(h * 512, (h + 1) * 512)
                nc.vector.tensor_tensor(out=accl[:, hs], in0=acc[:, hs], in1=acch[:, hs],
                                        op=ALU.subtract)
                for jc in range(4 * h, 4 * h + 4):
                    nc.tensor.matmul(csp[:, jc, 2, :], lhsT=acch[:, jc * P:(jc + 1) * P],
                                     rhs=onescol[:], start=True, stop=False)
                    nc.tensor.matmul(csp[:, jc, 2, :], lhsT=accl[:, jc * P:(jc + 1) * P],
                                     rhs=onescol[:], start=False, stop=True)
            nc.vector.tensor_reduce(out=tt[:], in_=csp[:], axis=AX.XY, op=ALU.add)
            nc.vector.reciprocal(out=bv[:], in_=tt[:])
            split(mvb, bv[:])

        def row_phase():
            bc = broadcast_bv()
            rsp = [bank(4 + g, [P, GT, NCOL], F32, "rsp") for g in range(2)]
            for t in range(NP):
                k = 0
                for jc in range(CC):
                    for eb in (ebh[t], ebl[t]):
                        nc.tensor.matmul(rsp[t // GT][:, t % GT, :], lhsT=eb[:, jc, :],
                                         rhs=mvb[:, jc, :],
                                         start=(k == 0), stop=(k == 2 * CC - 1))
                        k += 1
            for i in range(2 * NV):
                v = i // 2
                h = i % 2
                nc.vector.scalar_tensor_tensor(
                    out=junk[:], in0=ev[v][:, h * 512:(h + 1) * 512], scalar=1.0,
                    in1=bc[h][:], op0=ALU.mult, op1=ALU.mult,
                    accum_out=svh[:, v, h:h + 1])
                if i == MID - 1:
                    a_of_p_tiles(0, GT, rsp[0][:])
            nc.vector.tensor_reduce(out=s_all[:, NP:RT], in_=svh[:], axis=AX.X, op=ALU.add)
            nc.vector.reciprocal(out=a_all[:, NP:RT], in_=s_all[:, NP:RT])
            for i in range(EARLY):
                acc_step(i // 2, i % 2)
            a_of_p_tiles(GT, NP, rsp[1][:])

        def col_phase():
            col_open()
            for g in range(2):
                for jc in range(CC):
                    col_pe(jc, g)
            col_finish(EARLY)

        r32 = {}
        col_finish(2 * NV)
        for it in range(1, ITERS):
            row_phase()
            if it == ITERS - 1:
                for t in range(0, NP, 2):
                    r = big.tile([P, 2, COLS], F32, name="r32_%d" % t, offset=OFF_EB + t * 4 * KB)
                    if t < NP - REBUILT:
                        nc.sync.dma_start(out=r[:], in_=ov[:, t:t + 2, :])
                    r32[t] = r
            col_phase()

        bc = broadcast_bv()
        bcs = big.tile([P, COLS], F32, name="bcs", offset=OFF_BCS)
        for h in range(2):
            nc.scalar.copy(out=bcs[:, h * 512:(h + 1) * 512], in_=bc[h][:])
        g_pairs = [t for t in range(0, NP, 2) if t < 2 * GPAIRS]
        v_pairs = [t for t in range(0, NP - REBUILT, 2) if t >= 2 * GPAIRS]
        r_tiles = list(range(NP - REBUILT, NP))
        sum_banks = [(0, 1), (4, 5), (6, 7)]
        sums = {}

        def rebuild(i):
            t = r_tiles[i]
            for h in range(2):
                hs = slice(h * 512, (h + 1) * 512)
                esum = bank(sum_banks[i % 3][h], [P, 512], F32, "esum")
                nc.tensor.matmul(esum[:], lhsT=ident_b[:], rhs=eah[t][:, hs], start=True, stop=False)
                nc.tensor.matmul(esum[:], lhsT=ident_b[:], rhs=eal[t][:, hs], start=False, stop=True)
                sums[(t, h)] = esum

        for i in range(3):
            rebuild(i)
        for t in g_pairs:
            for e in range(2):
                nc.scalar.activation(out=r32[t][:, e, :], in_=r32[t][:, e, :], func=ACT.Copy,
                                     scale=a_all[:, t + e:t + e + 1])
        for t in g_pairs:
            for e in range(2):
                nc.gpsimd.tensor_tensor(out=r32[t][:, e, :], in0=r32[t][:, e, :], in1=bcs[:],
                                        op=ALU.mult)
            nc.scalar.dma_start(out=ov[:, t:t + 2, :], in_=r32[t][:])
        for v in range(NV):
            for h in range(2):
                hs = slice(h * 512, (h + 1) * 512)
                nc.vector.scalar_tensor_tensor(
                    out=ev[v][:, hs], in0=ev[v][:, hs], scalar=a_all[:, NP + v:NP + v + 1],
                    in1=bc[h][:], op0=ALU.mult, op1=ALU.mult)
            nc.sync.dma_start(out=ov[:, NP + v, :], in_=ev[v][:])
        for i, t in enumerate(r_tiles):
            for h in range(2):
                hs = slice(h * 512, (h + 1) * 512)
                nc.vector.scalar_tensor_tensor(
                    out=r32[t - t % 2][:, t % 2, hs], in0=sums[(t, h)][:],
                    scalar=a_all[:, t:t + 1], in1=bcs[:, hs], op0=ALU.mult, op1=ALU.mult)
            if i + 3 < REBUILT:
                rebuild(i + 3)
            if t % 2 == 1:
                nc.sync.dma_start(out=ov[:, t - 1:t + 1, :], in_=r32[t - 1][:])
        for t in v_pairs:
            for e in range(2):
                for h in range(2):
                    hs = slice(h * 512, (h + 1) * 512)
                    nc.vector.scalar_tensor_tensor(
                        out=r32[t][:, e, hs], in0=r32[t][:, e, hs],
                        scalar=a_all[:, t + e:t + e + 1], in1=bc[h][:],
                        op0=ALU.mult, op1=ALU.mult)
            nc.sync.dma_start(out=ov[:, t:t + 2, :], in_=r32[t][:])
